import numpy as np
import ml_dtypes


def mxq(x, axis, fmt="e4m3"):
    dtype, down = {"e4m3": (ml_dtypes.float8_e4m3fn, 7), "e5m2": (ml_dtypes.float8_e5m2, 14)}[fmt]
    v = np.moveaxis(np.asarray(x, np.float32).astype(ml_dtypes.bfloat16).astype(np.float64), axis, -1)
    blocks = v.reshape(v.shape[:-1] + (-1, 32))
    amax = np.abs(blocks).max(-1, keepdims=True)
    byte = np.maximum(np.where(amax > 0, np.frexp(amax)[1] - 1 + 127, 0) - down, 1)
    scale = np.exp2(byte - 127.0)
    codes = (blocks / scale).astype(np.float32).astype(dtype).astype(np.float64)
    return np.moveaxis((codes * scale).reshape(v.shape), -1, axis)


WIDE = False


def mx_kscale(k):
    if not WIDE:
        return np.ones(k)
    levels = np.array([10, -10, 5, -5, 0])
    a = np.random.permutation(np.resize(levels, k // 512 * 4)).reshape(k // 512, 4)
    idx = np.arange(k)
    return np.exp2(a[idx // 512, idx % 128 // 32])


BF16 = ml_dtypes.bfloat16


def bf(x):
    return np.asarray(x, np.float32).astype(BF16)


def f64(x):
    return np.asarray(x).astype(np.float64)


B, T, P, F, G, R, C, O = 256, 8, 1024, 512, 512, 128, 4, 10


def setup_inputs():
    s, t = mx_kscale(P + F), mx_kscale(G)
    u = np.roll(t, R)
    r0 = np.concatenate([1.0 / (np.sqrt(P + F) * s), [0.1]])[:, None]
    r1 = np.concatenate([1.5 / (np.sqrt(G) * t), [0.1]])[:, None]
    return {"primary_input": bf((np.random.standard_normal((B, T, P)) * s[:P]).reshape(B, T * P)),
            "prev": bf((np.maximum(np.random.standard_normal((B, T, F)), 0.0) * 0.9 * s[P:]).reshape(B, T * F)),
            "col": bf(np.array([float(np.random.randint(1, C))])),
            "W0": bf(np.random.standard_normal((P + F + 1, G)) * r0 * u),
            "b0": bf(np.random.standard_normal(G) * 0.2 * u),
            "W1": bf(np.random.standard_normal((G + 1, F)) * r1),
            "b1": bf(np.random.standard_normal(F) * 0.2)}


def reference(primary_input, prev, col, W0, b0, W1, b1):
    w0, w1, c = f64(W0), f64(W1), f64(col)
    inp = np.concatenate([f64(primary_input).reshape(B, T, P), f64(prev).reshape(B, T, F)], axis=-1)
    a = (mxq(inp, 2, "e4m3") @ mxq(w0[:P + F], 0, "e4m3")) + c * w0[P + F] + f64(b0)
    h = np.roll(np.maximum(a, 0.0).reshape(B, T * G), -R, axis=1).reshape(B, T, G)
    y = (mxq(h, 2, "e4m3") @ mxq(w1[:G], 0, "e4m3")) + c * w1[G] + f64(b1)
    return np.roll(np.maximum(y, 0.0).reshape(B, T * F), R, axis=1)

@@ -1,0 +1,261 @@
+from contextlib import ExitStack
+
+import concourse.mybir as mybir
+from concourse.masks import make_identity
+
+F32 = mybir.dt.float32
+BF16 = mybir.dt.bfloat16
+U32 = mybir.dt.uint32
+U8 = mybir.dt.uint8
+FP8X4 = mybir.dt.float8_e4m3fn_x4
+RELU = mybir.ActivationFunctionType.Relu
+ADD = mybir.AluOpType.add
+MAX = mybir.AluOpType.max
+
+FLOPS = 2 * 2048 * (1536 * 512 + 512 * 512)
+
+PINNED = True
+N_T = 3
+N_A = 3
+N_Y = 2
+D_H = 1
+D_Y = 2
+D_F = 3
+RELU_ENG = "SSSSSSSS"
+EV_ENG = "SSSSSSSSSSSSSSSSSSSSSSSS"
+HG_ENG = "VVVVVVVV"
+LOADS = ["P0","W0","X0","W1","W2","P1","X1","P2","X2","W3","P3","X3","P4","X4","P5","X5","P6","X6","P7","X7"]
+
+
+def tile_capsuleneuralnetwork_pa_kernel(tc, primary_input, prev, col, W0, b0, W1, b1, out):
+    nc = tc.nc
+    with ExitStack() as ctx:
+        keep = ctx.enter_context(tc.tile_pool(name="keep", bufs=1))
+        stage = ctx.enter_context(tc.tile_pool(name="stage", bufs=6))
+        ps_t = ctx.enter_context(tc.psum_pool(name="ps_t", bufs=N_T))
+        ps_a = ctx.enter_context(tc.psum_pool(name="ps_a", bufs=N_A))
+        ps_y = ctx.enter_context(tc.psum_pool(name="ps_y", bufs=N_Y))
+        if PINNED:
+            ctx.enter_context(tc.manual_schedule())
+
+        ident = keep.tile([128, 128], F32, name="ident")
+        make_identity(nc, ident[:])
+        bias_rows = keep.tile([128, 1024], BF16, name="bias_rows")
+        nc.vector.memset(bias_rows[:], 0.0)
+        col_ones = keep.tile([128, 128], BF16, name="col_ones")
+        nc.vector.memset(col_ones[:], 0.0)
+        nc.vector.memset(col_ones[32:64, :], 1.0)
+        col_sb = keep.tile([1, 1], BF16, name="col_sb")
+        nc.scalar.dma_start(out=col_sb[0:1, 0:1], in_=col.unsqueeze(0))
+        nc.scalar.dma_start(out=bias_rows[0:1, 0:512], in_=W0[1536:1537, :])
+        nc.scalar.dma_start(out=bias_rows[32:33, 0:512], in_=b0.unsqueeze(0))
+        nc.scalar.dma_start(out=bias_rows[0:1, 512:1024], in_=W1[512:513, :])
+        nc.scalar.dma_start(out=bias_rows[32:33, 512:1024], in_=b1.unsqueeze(0))
+
+        prim = [keep.tile([128, 2048], BF16, name="prim%d" % u) for u in range(8)]
+        prv = [keep.tile([128, 1024], BF16, name="prv%d" % u) for u in range(8)]
+        w_raw = [keep.tile([128, 4, 512], BF16, name="w_raw%d" % g) for g in range(4)]
+
+        for item in LOADS:
+            kind, k = item[0], int(item[1])
+            bh, v = divmod(k, 4)
+            if kind == "P":
+                nc.sync.dma_start(out=prim[k][:], in_=primary_input[128 * bh:128 * bh + 128, 2048 * v:2048 * v + 2048])
+            elif kind == "X":
+                nc.sync.dma_start(out=prv[k][:], in_=prev[128 * bh:128 * bh + 128, 1024 * v:1024 * v + 1024])
+            elif k < 3:
+                nc.sync.dma_start(
+                    out=w_raw[k][:].rearrange("p (u e) c -> p u e c", u=2),
+                    in_=W0[512 * k:512 * k + 512, :].rearrange("(u p e) c -> p u e c", u=2, p=128, e=2),
+                )
+            else:
+                nc.sync.dma_start(out=w_raw[3][:], in_=W1[0:512, :].rearrange("(c p) n -> p c n", p=128))
+
+        w_g = [keep.tile([128, 2048], BF16, name="w_g%d" % g, align_bytes=64) for g in range(4)]
+        w_c = [keep.tile([128, 512], U32, name="w_c%d" % g, align_bytes=64) for g in range(4)]
+        w_s = [keep.tile([128, 512], U8, name="w_s%d" % g, align_bytes=64) for g in range(4)]
+        x_c = [keep.tile([128, 3, 1024], U32, name="x_c%d" % b, align_bytes=64) for b in range(2)]
+        x_s = [keep.tile([128, 3, 1024], U8, name="x_s%d" % b, align_bytes=64) for b in range(2)]
+        h_t = [keep.tile([128, 4, 1024], BF16, name="h_t%d" % b) for b in range(2)]
+        h_g = [keep.tile([128, 4096], BF16, name="h_g%d" % b, align_bytes=64) for b in range(2)]
+        h_c = [keep.tile([128, 1024], U32, name="h_c%d" % b, align_bytes=64) for b in range(2)]
+        h_s = [keep.tile([128, 1024], U8, name="h_s%d" % b, align_bytes=64) for b in range(2)]
+        o_sb = [keep.tile([128, 4096], F32, name="o_sb%d" % b) for b in range(2)]
+        bias0 = keep.tile([128, 4], F32, name="bias0")
+        bias1 = keep.tile([128, 512], F32, name="bias1")
+
+        def regroup(eng, dst, src):
+            dst4 = dst.rearrange("p (c i t) -> p c t i", i=4, t=4)
+            src4 = src.rearrange("p t (c i) -> p c t i", i=4)
+            if eng == "V":
+                nc.vector.tensor_copy(out=dst4, in_=src4)
+            else:
+                nc.scalar.copy(out=dst4, in_=src4)
+
+        def quantise(codes, scales, src):
+            nc.vector.quantize_mx(out=codes.bitcast(FP8X4), scales=scales, in_=src)
+
+        banks = {}
+        x_g = {}
+
+        def tr(u):
+            if u > 7:
+                return
+            for g in range(3):
+                words = (prim[u] if g < 2 else prv[u])[:].bitcast(F32)
+                bank = ps_t.tile([128, 2, 2, 128], F32, name="bank", tag="tp")
+                banks[(u, g)] = bank
+                for t2 in range(2):
+                    for h in range(2):
+                        base = (512 * t2 + 256 * g + 128 * h) if g < 2 else (256 * t2 + 128 * h)
+                        nc.tensor.transpose(bank[:, t2, h, :], words[:, base:base + 128], ident[:])
+
+        def ev(u):
+            if u > 7:
+                return
+            for g in range(3):
+                grp = stage.tile([128, 1024], BF16, name="x_g", tag="x_g", align_bytes=64)
+                x_g[(u, g)] = grp
+                dst = grp[:].bitcast(F32).rearrange("p (t b h) -> p t b h", t=2, b=128, h=2)
+                src = banks[(u, g)][:].rearrange("p t h b -> p t b h")
+                if EV_ENG[3 * u + g] == "V":
+                    nc.vector.tensor_copy(out=dst, in_=src)
+                else:
+                    nc.scalar.copy(out=dst, in_=src)
+
+        def qx(u):
+            if u > 7:
+                return
+            bh, v = divmod(u, 4)
+            for g in range(3):
+                quantise(x_c[bh][:, g, 256 * v:256 * v + 256], x_s[bh][:, g, 256 * v:256 * v + 256], x_g[(u, g)][:])
+
+        def wr(g, eng="V"):
+            regroup(eng, w_g[g][:], w_raw[g][:])
+
+        def wq(g):
+            quantise(w_c[g][:], w_s[g][:], w_g[g][:])
+
+        def biases():
+            nc.vector.tensor_copy(out=col_ones[0:1, :], in_=col_sb[0:1, 0:1].to_broadcast([1, 128]))
+            pb0 = ps_y.tile([128, 4, 64], F32, name="pb0", tag="y")
+            for m in range(4):
+                nc.tensor.matmul(out=pb0[:, m, :], lhsT=bias_rows[:, 128 * m:128 * m + 128], rhs=col_ones[:, 0:64],
+                                 start=True, stop=True)
+            nc.vector.tensor_copy(out=bias0[:], in_=pb0[:, :, 0])
+            pb1 = ps_y.tile([128, 512], F32, name="pb1", tag="y")
+            nc.tensor.matmul(out=pb1[:], lhsT=col_ones[:], rhs=bias_rows[:, 512:1024], start=True, stop=True)
+            nc.vector.tensor_copy(out=bias1[:], in_=pb1[:])
+
+        def mx_group(dst, m, bh, c0, n):
+            for g in range(3):
+                nc.tensor.matmul_mx(
+                    out=dst,
+                    lhsT=w_c[g][:, 128 * m:128 * m + 128].bitcast(FP8X4),
+                    lhsT_scale=w_s[g][:, 128 * m:128 * m + 128],
+                    rhs=x_c[bh][:, g, c0:c0 + n].bitcast(FP8X4),
+                    rhs_scale=x_s[bh][:, g, c0:c0 + n],
+                    start=(g == 0),
+                    stop=(g == 2),
+                )
+
+        def layer1(w):
+            if w < 0 or w > 7:
+                return
+            bh, v = divmod(w, 4)
+            acc_a = ps_a.tile([128, 2, 256], F32, name="acc_a", tag="acc")
+            acc_b = ps_a.tile([128, 2, 256], F32, name="acc_b", tag="acc")
+            mx_group(acc_a[:, 0, :], 1, bh, 256 * v, 256)
+            mx_group(acc_a[:, 1, :], 2, bh, 256 * v, 256)
+            mx_group(acc_b[:, 0, :], 3, bh, 256 * v, 256)
+            if v < 3:
+                mx_group(acc_b[:, 1, :], 0, bh, 256 * v + 128, 256)
+            else:
+                mx_group(acc_b[:, 1, 0:128], 0, bh, 896, 128)
+                mx_group(acc_b[:, 1, 128:256], 0, bh, 0, 128)
+            for (src, m, c) in ((acc_a[:, 0, :], 1, 0), (acc_a[:, 1, :], 2, 1), (acc_b[:, 0, :], 3, 2), (acc_b[:, 1, :], 0, 3)):
+                nc.scalar.activation(out=h_t[bh][:, c, 256 * v:256 * v + 256], in_=src, func=RELU,
+                                     bias=bias0[:, m:m + 1], scale=1.0)
+
+        def hg(w):
+            if w < 0 or w > 7:
+                return
+            bh, v = divmod(w, 4)
+            regroup(HG_ENG[w], h_g[bh][:, 1024 * v:1024 * v + 1024], h_t[bh][:, :, 256 * v:256 * v + 256])
+
+        def qh(w):
+            if w < 0 or w > 7:
+                return
+            bh, v = divmod(w, 4)
+            quantise(h_c[bh][:, 256 * v:256 * v + 256], h_s[bh][:, 256 * v:256 * v + 256],
+                     h_g[bh][:, 1024 * v:1024 * v + 1024])
+
+        def layer2(w):
+            if w < 0 or w > 7:
+                return
+            bh, v = divmod(w, 4)
+            ys = []
+            for k in range(2):
+                t = 2 * v + k
+                y = ps_y.tile([128, 512], F32, name="y", tag="y")
+                ys.append(y)
+                nc.tensor.matmul_mx(
+                    out=y[:],
+                    lhsT=h_c[bh][:, 128 * t:128 * t + 128].bitcast(FP8X4),
+                    lhsT_scale=h_s[bh][:, 128 * t:128 * t + 128],
+                    rhs=w_c[3][:].bitcast(FP8X4),
+                    rhs_scale=w_s[3][:],
+                    start=True,
+                    stop=True,
+                )
+            for k in range(2):
+                t = 2 * v + k
+                pieces = [(512 * t + 128, 0, 512)] if t < 7 else [(3712, 0, 384), (0, 384, 128)]
+                for (dst0, src0, n) in pieces:
+                    nc.vector.tensor_tensor(out=o_sb[bh][:, dst0:dst0 + n], in0=ys[k][:, src0:src0 + n],
+                                            in1=bias1[:, src0:src0 + n], op=ADD)
+
+        def finish(w):
+            if w < 0 or w > 7:
+                return
+            bh, v = divmod(w, 4)
+            if v < 3:
+                spans = [(1024 * v + 128, 1024 * v + 1152)]
+            else:
+                spans = [(3200, 3712), (3712, 4096), (0, 128)]
+            for (a, b) in spans:
+                piece = o_sb[bh][:, a:b]
+                if RELU_ENG[w] == "S":
+                    nc.scalar.activation(out=piece, in_=piece, func=RELU)
+                elif RELU_ENG[w] == "V":
+                    nc.vector.tensor_scalar_max(out=piece, in0=piece, scalar1=0.0)
+                else:
+                    nc.gpsimd.tensor_scalar(out=piece, in0=piece, scalar1=0.0, scalar2=0.0, op0=MAX, op1=ADD)
+                nc.sync.dma_start(out=out[128 * bh:128 * bh + 128, a:b], in_=piece)
+
+        tr(0)
+        ev(0)
+        wr(0)
+        wr(1)
+        wq(0)
+        qx(0)
+        wq(1)
+        wr(2)
+        tr(1)
+        ev(1)
+        qx(1)
+        wq(2)
+        biases()
+        for s in range(8 + D_F + 1):
+            tr(s + 2)
+            ev(s + 2)
+            layer1(s)
+            hg(s - D_H)
+            if s == 0:
+                wr(3)
+            qx(s + 2)
+            if s == 0:
+                wq(3)
+            qh(s - D_H)
+            layer2(s - D_Y)
+            finish(s - D_F)

@@ -14,7 +14,7 @@ MAX = mybir.AluOpType.max
 
 FLOPS = 2 * 2048 * (1536 * 512 + 512 * 512)
 
-PINNED = True
+PINNED = False
 N_T = 3
 N_A = 3
 N_Y = 2

@@ -14,17 +14,17 @@ MAX = mybir.AluOpType.max
 
 FLOPS = 2 * 2048 * (1536 * 512 + 512 * 512)
 
-PINNED = False
+PINNED = True
 N_T = 3
 N_A = 3
 N_Y = 2
 D_H = 1
 D_Y = 2
 D_F = 3
-RELU_ENG = "SSSSSSSS"
+RELU_ENG = "GGGGGGGS"
 EV_ENG = "SSSSSSSSSSSSSSSSSSSSSSSS"
 HG_ENG = "VVVVVVVV"
-LOADS = ["P0","W0","X0","W1","W2","P1","X1","P2","X2","W3","P3","X3","P4","X4","P5","X5","P6","X6","P7","X7"]
+LOADS = ["W0","P0","W1","X0","W2","P1","X1","P2","X2","P3","X3","W3","P4","X4","P5","X5","P6","X6","P7","X7"]
 
 
 def tile_capsuleneuralnetwork_pa_kernel(tc, primary_input, prev, col, W0, b0, W1, b1, out):
@@ -233,28 +233,28 @@ def tile_capsuleneuralnetwork_pa_kernel(tc, primary_input, prev, col, W0, b0, W1
                     nc.gpsimd.tensor_scalar(out=piece, in0=piece, scalar1=0.0, scalar2=0.0, op0=MAX, op1=ADD)
                 nc.sync.dma_start(out=out[128 * bh:128 * bh + 128, a:b], in_=piece)
 
+        wr(0)
         tr(0)
         ev(0)
-        wr(0)
         wr(1)
         wq(0)
         qx(0)
-        wq(1)
         wr(2)
+        wq(1)
+        wq(2)
+        biases()
         tr(1)
         ev(1)
         qx(1)
-        wq(2)
-        biases()
         for s in range(8 + D_F + 1):
             tr(s + 2)
             ev(s + 2)
             layer1(s)
             hg(s - D_H)
-            if s == 0:
+            if s == 1:
                 wr(3)
             qx(s + 2)
-            if s == 0:
+            if s == 1:
                 wq(3)
             qh(s - D_H)
             layer2(s - D_Y)

@@ -21,7 +21,7 @@ N_Y = 2
 D_H = 1
 D_Y = 2
 D_F = 3
-RELU_ENG = "GGGGGGGS"
+RELU_ENG = "SSSSSSVV"
 EV_ENG = "SSSSSSSSSSSSSSSSSSSSSSSS"
 HG_ENG = "VVVVVVVV"
 LOADS = ["W0","P0","W1","X0","W2","P1","X1","P2","X2","P3","X3","W3","P4","X4","P5","X5","P6","X6","P7","X7"]
@@ -145,7 +145,7 @@ def tile_capsuleneuralnetwork_pa_kernel(tc, primary_input, prev, col, W0, b0, W1
             nc.vector.tensor_copy(out=bias0[:], in_=pb0[:, :, 0])
             pb1 = ps_y.tile([128, 512], F32, name="pb1", tag="y")
             nc.tensor.matmul(out=pb1[:], lhsT=col_ones[:], rhs=bias_rows[:, 512:1024], start=True, stop=True)
-            nc.vector.tensor_copy(out=bias1[:], in_=pb1[:])
+            nc.scalar.copy(out=bias1[:], in_=pb1[:])
 
         def mx_group(dst, m, bh, c0, n):
             for g in range(3):
@@ -258,4 +258,7 @@ def tile_capsuleneuralnetwork_pa_kernel(tc, primary_input, prev, col, W0, b0, W1
                 wq(3)
             qh(s - D_H)
             layer2(s - D_Y)
-            finish(s - D_F)
+            if 0 <= s - D_Y <= 7 and RELU_ENG[s - D_Y] == "V":
+                finish(s - D_Y)
+            if 0 <= s - D_F <= 7 and RELU_ENG[s - D_F] == "S":
+                finish(s - D_F)

@@ -10,21 +10,16 @@ U8 = mybir.dt.uint8
 FP8X4 = mybir.dt.float8_e4m3fn_x4
 RELU = mybir.ActivationFunctionType.Relu
 ADD = mybir.AluOpType.add
-MAX = mybir.AluOpType.max
 
 FLOPS = 2 * 2048 * (1536 * 512 + 512 * 512)
 
-PINNED = True
-N_T = 3
-N_A = 3
-N_Y = 2
-D_H = 1
-D_Y = 2
-D_F = 3
-RELU_ENG = "SSSSSSVV"
-EV_ENG = "SSSSSSSSSSSSSSSSSSSSSSSS"
-HG_ENG = "VVVVVVVV"
-LOADS = ["W0","P0","W1","X0","W2","P1","X1","P2","X2","P3","X3","W3","P4","X4","P5","X5","P6","X6","P7","X7"]
+UNITS = 8
+PASSES = 3
+
+AHEAD_X = 2
+LAG_H = 1
+LAG_Y = 2
+LAG_OUT = 3
 
 
 def tile_capsuleneuralnetwork_pa_kernel(tc, primary_input, prev, col, W0, b0, W1, b1, out):
@@ -32,50 +27,63 @@ def tile_capsuleneuralnetwork_pa_kernel(tc, primary_input, prev, col, W0, b0, W1
     with ExitStack() as ctx:
         keep = ctx.enter_context(tc.tile_pool(name="keep", bufs=1))
         stage = ctx.enter_context(tc.tile_pool(name="stage", bufs=6))
-        ps_t = ctx.enter_context(tc.psum_pool(name="ps_t", bufs=N_T))
-        ps_a = ctx.enter_context(tc.psum_pool(name="ps_a", bufs=N_A))
-        ps_y = ctx.enter_context(tc.psum_pool(name="ps_y", bufs=N_Y))
-        if PINNED:
-            ctx.enter_context(tc.manual_schedule())
+        ps_t = ctx.enter_context(tc.psum_pool(name="ps_t", bufs=3))
+        ps_a = ctx.enter_context(tc.psum_pool(name="ps_a", bufs=3))
+        ps_y = ctx.enter_context(tc.psum_pool(name="ps_y", bufs=2))
+        ctx.enter_context(tc.manual_schedule())
 
         ident = keep.tile([128, 128], F32, name="ident")
         make_identity(nc, ident[:])
         bias_rows = keep.tile([128, 1024], BF16, name="bias_rows")
         nc.vector.memset(bias_rows[:], 0.0)
         col_ones = keep.tile([128, 128], BF16, name="col_ones")
-        nc.vector.memset(col_ones[:], 0.0)
-        nc.vector.memset(col_ones[32:64, :], 1.0)
+        nc.gpsimd.memset(col_ones[:], 0.0)
+        nc.gpsimd.memset(col_ones[32:64, :], 1.0)
         col_sb = keep.tile([1, 1], BF16, name="col_sb")
         nc.scalar.dma_start(out=col_sb[0:1, 0:1], in_=col.unsqueeze(0))
+        nc.gpsimd.tensor_copy(out=col_ones[0:1, :], in_=col_sb[0:1, 0:1].to_broadcast([1, 128]))
         nc.scalar.dma_start(out=bias_rows[0:1, 0:512], in_=W0[1536:1537, :])
         nc.scalar.dma_start(out=bias_rows[32:33, 0:512], in_=b0.unsqueeze(0))
         nc.scalar.dma_start(out=bias_rows[0:1, 512:1024], in_=W1[512:513, :])
         nc.scalar.dma_start(out=bias_rows[32:33, 512:1024], in_=b1.unsqueeze(0))
 
-        prim = [keep.tile([128, 2048], BF16, name="prim%d" % u) for u in range(8)]
-        prv = [keep.tile([128, 1024], BF16, name="prv%d" % u) for u in range(8)]
+        prim = [keep.tile([128, 2048], BF16, name="prim%d" % u) for u in range(UNITS)]
+        prv = [keep.tile([128, 1024], BF16, name="prv%d" % u) for u in range(UNITS)]
         w_raw = [keep.tile([128, 4, 512], BF16, name="w_raw%d" % g) for g in range(4)]
 
-        for item in LOADS:
-            kind, k = item[0], int(item[1])
-            bh, v = divmod(k, 4)
-            if kind == "P":
-                nc.sync.dma_start(out=prim[k][:], in_=primary_input[128 * bh:128 * bh + 128, 2048 * v:2048 * v + 2048])
-            elif kind == "X":
-                nc.sync.dma_start(out=prv[k][:], in_=prev[128 * bh:128 * bh + 128, 1024 * v:1024 * v + 1024])
-            elif k < 3:
-                nc.sync.dma_start(
-                    out=w_raw[k][:].rearrange("p (u e) c -> p u e c", u=2),
-                    in_=W0[512 * k:512 * k + 512, :].rearrange("(u p e) c -> p u e c", u=2, p=128, e=2),
-                )
-            else:
-                nc.sync.dma_start(out=w_raw[3][:], in_=W1[0:512, :].rearrange("(c p) n -> p c n", p=128))
+        def load_primary(u):
+            half, v = divmod(u, 4)
+            nc.sync.dma_start(out=prim[u][:],
+                              in_=primary_input[128 * half:128 * half + 128, 2048 * v:2048 * v + 2048])
+
+        def load_prev(u):
+            half, v = divmod(u, 4)
+            nc.sync.dma_start(out=prv[u][:], in_=prev[128 * half:128 * half + 128, 1024 * v:1024 * v + 1024])
+
+        def load_w0(g):
+            nc.sync.dma_start(
+                out=w_raw[g][:].rearrange("p (u e) c -> p u e c", u=2),
+                in_=W0[512 * g:512 * g + 512, :].rearrange("(u p e) c -> p u e c", u=2, p=128, e=2),
+            )
+
+        load_primary(0)
+        load_w0(0)
+        load_prev(0)
+        load_w0(1)
+        load_w0(2)
+        for u in (1, 2):
+            load_primary(u)
+            load_prev(u)
+        nc.sync.dma_start(out=w_raw[3][:], in_=W1[0:512, :].rearrange("(c p) n -> p c n", p=128))
+        for u in range(3, UNITS):
+            load_primary(u)
+            load_prev(u)
 
         w_g = [keep.tile([128, 2048], BF16, name="w_g%d" % g, align_bytes=64) for g in range(4)]
         w_c = [keep.tile([128, 512], U32, name="w_c%d" % g, align_bytes=64) for g in range(4)]
         w_s = [keep.tile([128, 512], U8, name="w_s%d" % g, align_bytes=64) for g in range(4)]
-        x_c = [keep.tile([128, 3, 1024], U32, name="x_c%d" % b, align_bytes=64) for b in range(2)]
-        x_s = [keep.tile([128, 3, 1024], U8, name="x_s%d" % b, align_bytes=64) for b in range(2)]
+        x_c = [keep.tile([128, PASSES, 1024], U32, name="x_c%d" % b, align_bytes=64) for b in range(2)]
+        x_s = [keep.tile([128, PASSES, 1024], U8, name="x_s%d" % b, align_bytes=64) for b in range(2)]
         h_t = [keep.tile([128, 4, 1024], BF16, name="h_t%d" % b) for b in range(2)]
         h_g = [keep.tile([128, 4096], BF16, name="h_g%d" % b, align_bytes=64) for b in range(2)]
         h_c = [keep.tile([128, 1024], U32, name="h_c%d" % b, align_bytes=64) for b in range(2)]
@@ -84,13 +92,11 @@ def tile_capsuleneuralnetwork_pa_kernel(tc, primary_input, prev, col, W0, b0, W1
         bias0 = keep.tile([128, 4], F32, name="bias0")
         bias1 = keep.tile([128, 512], F32, name="bias1")
 
-        def regroup(eng, dst, src):
-            dst4 = dst.rearrange("p (c i t) -> p c t i", i=4, t=4)
-            src4 = src.rearrange("p t (c i) -> p c t i", i=4)
-            if eng == "V":
-                nc.vector.tensor_copy(out=dst4, in_=src4)
-            else:
-                nc.scalar.copy(out=dst4, in_=src4)
+        def regroup(dst, src):
+            nc.vector.tensor_copy(
+                out=dst.rearrange("p (c i t) -> p c t i", i=4, t=4),
+                in_=src.rearrange("p t (c i) -> p c t i", i=4),
+            )
 
         def quantise(codes, scales, src):
             nc.vector.quantize_mx(out=codes.bitcast(FP8X4), scales=scales, in_=src)
@@ -98,10 +104,8 @@ def tile_capsuleneuralnetwork_pa_kernel(tc, primary_input, prev, col, W0, b0, W1
         banks = {}
         x_g = {}
 
-        def tr(u):
-            if u > 7:
-                return
-            for g in range(3):
+        def transpose_inputs(u):
+            for g in range(PASSES):
                 words = (prim[u] if g < 2 else prv[u])[:].bitcast(F32)
                 bank = ps_t.tile([128, 2, 2, 128], F32, name="bank", tag="tp")
                 banks[(u, g)] = bank
@@ -110,90 +114,76 @@ def tile_capsuleneuralnetwork_pa_kernel(tc, primary_input, prev, col, W0, b0, W1
                         base = (512 * t2 + 256 * g + 128 * h) if g < 2 else (256 * t2 + 128 * h)
                         nc.tensor.transpose(bank[:, t2, h, :], words[:, base:base + 128], ident[:])
 
-        def ev(u):
-            if u > 7:
-                return
-            for g in range(3):
+        def copy_inputs(u):
+            for g in range(PASSES):
                 grp = stage.tile([128, 1024], BF16, name="x_g", tag="x_g", align_bytes=64)
                 x_g[(u, g)] = grp
-                dst = grp[:].bitcast(F32).rearrange("p (t b h) -> p t b h", t=2, b=128, h=2)
-                src = banks[(u, g)][:].rearrange("p t h b -> p t b h")
-                if EV_ENG[3 * u + g] == "V":
-                    nc.vector.tensor_copy(out=dst, in_=src)
-                else:
-                    nc.scalar.copy(out=dst, in_=src)
+                nc.scalar.copy(
+                    out=grp[:].bitcast(F32).rearrange("p (t b h) -> p t b h", t=2, b=128, h=2),
+                    in_=banks[(u, g)][:].rearrange("p t h b -> p t b h"),
+                )
 
-        def qx(u):
-            if u > 7:
-                return
-            bh, v = divmod(u, 4)
-            for g in range(3):
-                quantise(x_c[bh][:, g, 256 * v:256 * v + 256], x_s[bh][:, g, 256 * v:256 * v + 256], x_g[(u, g)][:])
+        def quantise_inputs(u):
+            half, v = divmod(u, 4)
+            for g in range(PASSES):
+                quantise(x_c[half][:, g, 256 * v:256 * v + 256], x_s[half][:, g, 256 * v:256 * v + 256],
+                         x_g[(u, g)][:])
 
-        def wr(g, eng="V"):
-            regroup(eng, w_g[g][:], w_raw[g][:])
+        def regroup_weights(g):
+            regroup(w_g[g][:], w_raw[g][:])
 
-        def wq(g):
+        def quantise_weights(g):
             quantise(w_c[g][:], w_s[g][:], w_g[g][:])
 
         def biases():
-            nc.vector.tensor_copy(out=col_ones[0:1, :], in_=col_sb[0:1, 0:1].to_broadcast([1, 128]))
             pb0 = ps_y.tile([128, 4, 64], F32, name="pb0", tag="y")
             for m in range(4):
                 nc.tensor.matmul(out=pb0[:, m, :], lhsT=bias_rows[:, 128 * m:128 * m + 128], rhs=col_ones[:, 0:64],
                                  start=True, stop=True)
-            nc.vector.tensor_copy(out=bias0[:], in_=pb0[:, :, 0])
+            nc.scalar.copy(out=bias0[:], in_=pb0[:, :, 0])
             pb1 = ps_y.tile([128, 512], F32, name="pb1", tag="y")
             nc.tensor.matmul(out=pb1[:], lhsT=col_ones[:], rhs=bias_rows[:, 512:1024], start=True, stop=True)
             nc.scalar.copy(out=bias1[:], in_=pb1[:])
 
-        def mx_group(dst, m, bh, c0, n):
-            for g in range(3):
+        def layer1_group(dst, m, half, c0, n):
+            for g in range(PASSES):
                 nc.tensor.matmul_mx(
                     out=dst,
                     lhsT=w_c[g][:, 128 * m:128 * m + 128].bitcast(FP8X4),
                     lhsT_scale=w_s[g][:, 128 * m:128 * m + 128],
-                    rhs=x_c[bh][:, g, c0:c0 + n].bitcast(FP8X4),
-                    rhs_scale=x_s[bh][:, g, c0:c0 + n],
+                    rhs=x_c[half][:, g, c0:c0 + n].bitcast(FP8X4),
+                    rhs_scale=x_s[half][:, g, c0:c0 + n],
                     start=(g == 0),
-                    stop=(g == 2),
+                    stop=(g == PASSES - 1),
                 )
 
         def layer1(w):
-            if w < 0 or w > 7:
-                return
-            bh, v = divmod(w, 4)
+            half, v = divmod(w, 4)
             acc_a = ps_a.tile([128, 2, 256], F32, name="acc_a", tag="acc")
             acc_b = ps_a.tile([128, 2, 256], F32, name="acc_b", tag="acc")
-            mx_group(acc_a[:, 0, :], 1, bh, 256 * v, 256)
-            mx_group(acc_a[:, 1, :], 2, bh, 256 * v, 256)
-            mx_group(acc_b[:, 0, :], 3, bh, 256 * v, 256)
+            layer1_group(acc_a[:, 0, :], 1, half, 256 * v, 256)
+            layer1_group(acc_a[:, 1, :], 2, half, 256 * v, 256)
+            layer1_group(acc_b[:, 0, :], 3, half, 256 * v, 256)
             if v < 3:
-                mx_group(acc_b[:, 1, :], 0, bh, 256 * v + 128, 256)
+                layer1_group(acc_b[:, 1, :], 0, half, 256 * v + 128, 256)
             else:
-                mx_group(acc_b[:, 1, 0:128], 0, bh, 896, 128)
-                mx_group(acc_b[:, 1, 128:256], 0, bh, 0, 128)
+                layer1_group(acc_b[:, 1, 0:128], 0, half, 896, 128)
+                layer1_group(acc_b[:, 1, 128:256], 0, half, 0, 128)
             for (src, m, c) in ((acc_a[:, 0, :], 1, 0), (acc_a[:, 1, :], 2, 1), (acc_b[:, 0, :], 3, 2), (acc_b[:, 1, :], 0, 3)):
-                nc.scalar.activation(out=h_t[bh][:, c, 256 * v:256 * v + 256], in_=src, func=RELU,
+                nc.scalar.activation(out=h_t[half][:, c, 256 * v:256 * v + 256], in_=src, func=RELU,
                                      bias=bias0[:, m:m + 1], scale=1.0)
 
-        def hg(w):
-            if w < 0 or w > 7:
-                return
-            bh, v = divmod(w, 4)
-            regroup(HG_ENG[w], h_g[bh][:, 1024 * v:1024 * v + 1024], h_t[bh][:, :, 256 * v:256 * v + 256])
+        def regroup_h(w):
+            half, v = divmod(w, 4)
+            regroup(h_g[half][:, 1024 * v:1024 * v + 1024], h_t[half][:, :, 256 * v:256 * v + 256])
 
-        def qh(w):
-            if w < 0 or w > 7:
-                return
-            bh, v = divmod(w, 4)
-            quantise(h_c[bh][:, 256 * v:256 * v + 256], h_s[bh][:, 256 * v:256 * v + 256],
-                     h_g[bh][:, 1024 * v:1024 * v + 1024])
+        def quantise_h(w):
+            half, v = divmod(w, 4)
+            quantise(h_c[half][:, 256 * v:256 * v + 256], h_s[half][:, 256 * v:256 * v + 256],
+                     h_g[half][:, 1024 * v:1024 * v + 1024])
 
         def layer2(w):
-            if w < 0 or w > 7:
-                return
-            bh, v = divmod(w, 4)
+            half, v = divmod(w, 4)
             ys = []
             for k in range(2):
                 t = 2 * v + k
@@ -201,8 +191,8 @@ def tile_capsuleneuralnetwork_pa_kernel(tc, primary_input, prev, col, W0, b0, W1
                 ys.append(y)
                 nc.tensor.matmul_mx(
                     out=y[:],
-                    lhsT=h_c[bh][:, 128 * t:128 * t + 128].bitcast(FP8X4),
-                    lhsT_scale=h_s[bh][:, 128 * t:128 * t + 128],
+                    lhsT=h_c[half][:, 128 * t:128 * t + 128].bitcast(FP8X4),
+                    lhsT_scale=h_s[half][:, 128 * t:128 * t + 128],
                     rhs=w_c[3][:].bitcast(FP8X4),
                     rhs_scale=w_s[3][:],
                     start=True,
@@ -212,53 +202,51 @@ def tile_capsuleneuralnetwork_pa_kernel(tc, primary_input, prev, col, W0, b0, W1
                 t = 2 * v + k
                 pieces = [(512 * t + 128, 0, 512)] if t < 7 else [(3712, 0, 384), (0, 384, 128)]
                 for (dst0, src0, n) in pieces:
-                    nc.vector.tensor_tensor(out=o_sb[bh][:, dst0:dst0 + n], in0=ys[k][:, src0:src0 + n],
+                    nc.vector.tensor_tensor(out=o_sb[half][:, dst0:dst0 + n], in0=ys[k][:, src0:src0 + n],
                                             in1=bias1[:, src0:src0 + n], op=ADD)
 
         def finish(w):
-            if w < 0 or w > 7:
-                return
-            bh, v = divmod(w, 4)
+            half, v = divmod(w, 4)
             if v < 3:
                 spans = [(1024 * v + 128, 1024 * v + 1152)]
             else:
                 spans = [(3200, 3712), (3712, 4096), (0, 128)]
             for (a, b) in spans:
-                piece = o_sb[bh][:, a:b]
-                if RELU_ENG[w] == "S":
-                    nc.scalar.activation(out=piece, in_=piece, func=RELU)
-                elif RELU_ENG[w] == "V":
-                    nc.vector.tensor_scalar_max(out=piece, in0=piece, scalar1=0.0)
-                else:
-                    nc.gpsimd.tensor_scalar(out=piece, in0=piece, scalar1=0.0, scalar2=0.0, op0=MAX, op1=ADD)
-                nc.sync.dma_start(out=out[128 * bh:128 * bh + 128, a:b], in_=piece)
+                piece = o_sb[half][:, a:b]
+                nc.scalar.activation(out=piece, in_=piece, func=RELU)
+                nc.sync.dma_start(out=out[128 * half:128 * half + 128, a:b], in_=piece)
 
-        wr(0)
-        tr(0)
-        ev(0)
-        wr(1)
-        wq(0)
-        qx(0)
-        wr(2)
-        wq(1)
-        wq(2)
+        transpose_inputs(0)
+        copy_inputs(0)
         biases()
-        tr(1)
-        ev(1)
-        qx(1)
-        for s in range(8 + D_F + 1):
-            tr(s + 2)
-            ev(s + 2)
-            layer1(s)
-            hg(s - D_H)
-            if s == 1:
-                wr(3)
-            qx(s + 2)
-            if s == 1:
-                wq(3)
-            qh(s - D_H)
-            layer2(s - D_Y)
-            if 0 <= s - D_Y <= 7 and RELU_ENG[s - D_Y] == "V":
-                finish(s - D_Y)
-            if 0 <= s - D_F <= 7 and RELU_ENG[s - D_F] == "S":
-                finish(s - D_F)
+        regroup_weights(0)
+        regroup_weights(1)
+        quantise_weights(0)
+        quantise_inputs(0)
+        regroup_weights(2)
+        quantise_weights(1)
+        quantise_weights(2)
+        transpose_inputs(1)
+        copy_inputs(1)
+        quantise_inputs(1)
+
+        for s in range(UNITS + LAG_OUT):
+            if s + AHEAD_X < UNITS:
+                transpose_inputs(s + AHEAD_X)
+                copy_inputs(s + AHEAD_X)
+            if s < UNITS:
+                layer1(s)
+            if 0 <= s - LAG_H < UNITS:
+                regroup_h(s - LAG_H)
+            if s == 0:
+                regroup_weights(3)
+            if s + AHEAD_X < UNITS:
+                quantise_inputs(s + AHEAD_X)
+            if s == 0:
+                quantise_weights(3)
+            if 0 <= s - LAG_H < UNITS:
+                quantise_h(s - LAG_H)
+            if 0 <= s - LAG_Y < UNITS:
+                layer2(s - LAG_Y)
+            if 0 <= s - LAG_OUT < UNITS:
+                finish(s - LAG_OUT)

@@ -118,10 +118,12 @@ def tile_capsuleneuralnetwork_pa_kernel(tc, primary_input, prev, col, W0, b0, W1
             for g in range(PASSES):
                 grp = stage.tile([128, 1024], BF16, name="x_g", tag="x_g", align_bytes=64)
                 x_g[(u, g)] = grp
-                nc.scalar.copy(
-                    out=grp[:].bitcast(F32).rearrange("p (t b h) -> p t b h", t=2, b=128, h=2),
-                    in_=banks[(u, g)][:].rearrange("p t h b -> p t b h"),
-                )
+                dst = grp[:].bitcast(F32).rearrange("p (t b h) -> p t b h", t=2, b=128, h=2)
+                src = banks[(u, g)][:].rearrange("p t h b -> p t b h")
+                if g == 2 and u >= 3:
+                    nc.vector.tensor_copy(out=dst, in_=src)
+                else:
+                    nc.scalar.copy(out=dst, in_=src)
 
         def quantise_inputs(u):
             half, v = divmod(u, 4)

@@ -209,10 +209,11 @@ def tile_capsuleneuralnetwork_pa_kernel(tc, primary_input, prev, col, W0, b0, W1
 
         def finish(w):
             half, v = divmod(w, 4)
+            spans = [(1024 * v + 128, 1024 * v + 640)]
             if v < 3:
-                spans = [(1024 * v + 128, 1024 * v + 1152)]
+                spans.append((1024 * v + 640, 1024 * v + 1152))
             else:
-                spans = [(3200, 3712), (3712, 4096), (0, 128)]
+                spans.extend([(3712, 4096), (0, 128)])
             for (a, b) in spans:
                 piece = o_sb[half][:, a:b]
                 nc.scalar.activation(out=piece, in_=piece, func=RELU)

from contextlib import ExitStack

import concourse.mybir as mybir
from concourse.masks import make_identity

F32 = mybir.dt.float32
BF16 = mybir.dt.bfloat16
U32 = mybir.dt.uint32
U8 = mybir.dt.uint8
FP8X4 = mybir.dt.float8_e4m3fn_x4
RELU = mybir.ActivationFunctionType.Relu
ADD = mybir.AluOpType.add

FLOPS = 2 * 2048 * (1536 * 512 + 512 * 512)

UNITS = 8
PASSES = 3

AHEAD_X = 2
LAG_H = 1
LAG_Y = 2
LAG_OUT = 3


def tile_capsuleneuralnetwork_pa_kernel(tc, primary_input, prev, col, W0, b0, W1, b1, out):
    nc = tc.nc
    with ExitStack() as ctx:
        keep = ctx.enter_context(tc.tile_pool(name="keep", bufs=1))
        stage = ctx.enter_context(tc.tile_pool(name="stage", bufs=6))
        ps_t = ctx.enter_context(tc.psum_pool(name="ps_t", bufs=3))
        ps_a = ctx.enter_context(tc.psum_pool(name="ps_a", bufs=3))
        ps_y = ctx.enter_context(tc.psum_pool(name="ps_y", bufs=2))
        ctx.enter_context(tc.manual_schedule())

        ident = keep.tile([128, 128], F32, name="ident")
        make_identity(nc, ident[:])
        bias_rows = keep.tile([128, 1024], BF16, name="bias_rows")
        nc.vector.memset(bias_rows[:], 0.0)
        col_ones = keep.tile([128, 128], BF16, name="col_ones")
        nc.gpsimd.memset(col_ones[:], 0.0)
        nc.gpsimd.memset(col_ones[32:64, :], 1.0)
        col_sb = keep.tile([1, 1], BF16, name="col_sb")
        nc.scalar.dma_start(out=col_sb[0:1, 0:1], in_=col.unsqueeze(0))
        nc.gpsimd.tensor_copy(out=col_ones[0:1, :], in_=col_sb[0:1, 0:1].to_broadcast([1, 128]))
        nc.scalar.dma_start(out=bias_rows[0:1, 0:512], in_=W0[1536:1537, :])
        nc.scalar.dma_start(out=bias_rows[32:33, 0:512], in_=b0.unsqueeze(0))
        nc.scalar.dma_start(out=bias_rows[0:1, 512:1024], in_=W1[512:513, :])
        nc.scalar.dma_start(out=bias_rows[32:33, 512:1024], in_=b1.unsqueeze(0))

        prim = [keep.tile([128, 2048], BF16, name="prim%d" % u) for u in range(UNITS)]
        prv = [keep.tile([128, 1024], BF16, name="prv%d" % u) for u in range(UNITS)]
        w_raw = [keep.tile([128, 4, 512], BF16, name="w_raw%d" % g) for g in range(4)]

        def load_primary(u):
            half, v = divmod(u, 4)
            nc.sync.dma_start(out=prim[u][:],
                              in_=primary_input[128 * half:128 * half + 128, 2048 * v:2048 * v + 2048])

        def load_prev(u):
            half, v = divmod(u, 4)
            nc.sync.dma_start(out=prv[u][:], in_=prev[128 * half:128 * half + 128, 1024 * v:1024 * v + 1024])

        def load_w0(g):
            nc.sync.dma_start(
                out=w_raw[g][:].rearrange("p (u e) c -> p u e c", u=2),
                in_=W0[512 * g:512 * g + 512, :].rearrange("(u p e) c -> p u e c", u=2, p=128, e=2),
            )

        load_primary(0)
        load_w0(0)
        load_prev(0)
        load_w0(1)
        load_w0(2)
        for u in (1, 2):
            load_primary(u)
            load_prev(u)
        nc.sync.dma_start(out=w_raw[3][:], in_=W1[0:512, :].rearrange("(c p) n -> p c n", p=128))
        for u in range(3, UNITS):
            load_primary(u)
            load_prev(u)

        w_g = [keep.tile([128, 2048], BF16, name="w_g%d" % g, align_bytes=64) for g in range(4)]
        w_c = [keep.tile([128, 512], U32, name="w_c%d" % g, align_bytes=64) for g in range(4)]
        w_s = [keep.tile([128, 512], U8, name="w_s%d" % g, align_bytes=64) for g in range(4)]
        x_c = [keep.tile([128, PASSES, 1024], U32, name="x_c%d" % b, align_bytes=64) for b in range(2)]
        x_s = [keep.tile([128, PASSES, 1024], U8, name="x_s%d" % b, align_bytes=64) for b in range(2)]
        h_t = [keep.tile([128, 4, 1024], BF16, name="h_t%d" % b) for b in range(2)]
        h_g = [keep.tile([128, 4096], BF16, name="h_g%d" % b, align_bytes=64) for b in range(2)]
        h_c = [keep.tile([128, 1024], U32, name="h_c%d" % b, align_bytes=64) for b in range(2)]
        h_s = [keep.tile([128, 1024], U8, name="h_s%d" % b, align_bytes=64) for b in range(2)]
        o_sb = [keep.tile([128, 4096], F32, name="o_sb%d" % b) for b in range(2)]
        bias0 = keep.tile([128, 4], F32, name="bias0")
        bias1 = keep.tile([128, 512], F32, name="bias1")

        def regroup(dst, src):
            nc.vector.tensor_copy(
                out=dst.rearrange("p (c i t) -> p c t i", i=4, t=4),
                in_=src.rearrange("p t (c i) -> p c t i", i=4),
            )

        def quantise(codes, scales, src):
            nc.vector.quantize_mx(out=codes.bitcast(FP8X4), scales=scales, in_=src)

        banks = {}
        x_g = {}

        def transpose_inputs(u):
            for g in range(PASSES):
                words = (prim[u] if g < 2 else prv[u])[:].bitcast(F32)
                bank = ps_t.tile([128, 2, 2, 128], F32, name="bank", tag="tp")
                banks[(u, g)] = bank
                for t2 in range(2):
                    for h in range(2):
                        base = (512 * t2 + 256 * g + 128 * h) if g < 2 else (256 * t2 + 128 * h)
                        nc.tensor.transpose(bank[:, t2, h, :], words[:, base:base + 128], ident[:])

        def copy_inputs(u):
            for g in range(PASSES):
                grp = stage.tile([128, 1024], BF16, name="x_g", tag="x_g", align_bytes=64)
                x_g[(u, g)] = grp
                dst = grp[:].bitcast(F32).rearrange("p (t b h) -> p t b h", t=2, b=128, h=2)
                src = banks[(u, g)][:].rearrange("p t h b -> p t b h")
                if g == 2 and u >= 3:
                    nc.vector.tensor_copy(out=dst, in_=src)
                else:
                    nc.scalar.copy(out=dst, in_=src)

        def quantise_inputs(u):
            half, v = divmod(u, 4)
            for g in range(PASSES):
                quantise(x_c[half][:, g, 256 * v:256 * v + 256], x_s[half][:, g, 256 * v:256 * v + 256],
                         x_g[(u, g)][:])

        def regroup_weights(g):
            regroup(w_g[g][:], w_raw[g][:])

        def quantise_weights(g):
            quantise(w_c[g][:], w_s[g][:], w_g[g][:])

        def biases():
            pb0 = ps_y.tile([128, 4, 64], F32, name="pb0", tag="y")
            for m in range(4):
                nc.tensor.matmul(out=pb0[:, m, :], lhsT=bias_rows[:, 128 * m:128 * m + 128], rhs=col_ones[:, 0:64],
                                 start=True, stop=True)
            nc.scalar.copy(out=bias0[:], in_=pb0[:, :, 0])
            pb1 = ps_y.tile([128, 512], F32, name="pb1", tag="y")
            nc.tensor.matmul(out=pb1[:], lhsT=col_ones[:], rhs=bias_rows[:, 512:1024], start=True, stop=True)
            nc.scalar.copy(out=bias1[:], in_=pb1[:])

        def layer1_group(dst, m, half, c0, n):
            for g in range(PASSES):
                nc.tensor.matmul_mx(
                    out=dst,
                    lhsT=w_c[g][:, 128 * m:128 * m + 128].bitcast(FP8X4),
                    lhsT_scale=w_s[g][:, 128 * m:128 * m + 128],
                    rhs=x_c[half][:, g, c0:c0 + n].bitcast(FP8X4),
                    rhs_scale=x_s[half][:, g, c0:c0 + n],
                    start=(g == 0),
                    stop=(g == PASSES - 1),
                )

        def layer1(w):
            half, v = divmod(w, 4)
            acc_a = ps_a.tile([128, 2, 256], F32, name="acc_a", tag="acc")
            acc_b = ps_a.tile([128, 2, 256], F32, name="acc_b", tag="acc")
            layer1_group(acc_a[:, 0, :], 1, half, 256 * v, 256)
            layer1_group(acc_a[:, 1, :], 2, half, 256 * v, 256)
            layer1_group(acc_b[:, 0, :], 3, half, 256 * v, 256)
            if v < 3:
                layer1_group(acc_b[:, 1, :], 0, half, 256 * v + 128, 256)
            else:
                layer1_group(acc_b[:, 1, 0:128], 0, half, 896, 128)
                layer1_group(acc_b[:, 1, 128:256], 0, half, 0, 128)
            for (src, m, c) in ((acc_a[:, 0, :], 1, 0), (acc_a[:, 1, :], 2, 1), (acc_b[:, 0, :], 3, 2), (acc_b[:, 1, :], 0, 3)):
                nc.scalar.activation(out=h_t[half][:, c, 256 * v:256 * v + 256], in_=src, func=RELU,
                                     bias=bias0[:, m:m + 1], scale=1.0)

        def regroup_h(w):
            half, v = divmod(w, 4)
            regroup(h_g[half][:, 1024 * v:1024 * v + 1024], h_t[half][:, :, 256 * v:256 * v + 256])

        def quantise_h(w):
            half, v = divmod(w, 4)
            quantise(h_c[half][:, 256 * v:256 * v + 256], h_s[half][:, 256 * v:256 * v + 256],
                     h_g[half][:, 1024 * v:1024 * v + 1024])

        def layer2(w):
            half, v = divmod(w, 4)
            ys = []
            for k in range(2):
                t = 2 * v + k
                y = ps_y.tile([128, 512], F32, name="y", tag="y")
                ys.append(y)
                nc.tensor.matmul_mx(
                    out=y[:],
                    lhsT=h_c[half][:, 128 * t:128 * t + 128].bitcast(FP8X4),
                    lhsT_scale=h_s[half][:, 128 * t:128 * t + 128],
                    rhs=w_c[3][:].bitcast(FP8X4),
                    rhs_scale=w_s[3][:],
                    start=True,
                    stop=True,
                )
            for k in range(2):
                t = 2 * v + k
                pieces = [(512 * t + 128, 0, 512)] if t < 7 else [(3712, 0, 384), (0, 384, 128)]
                for (dst0, src0, n) in pieces:
                    nc.vector.tensor_tensor(out=o_sb[half][:, dst0:dst0 + n], in0=ys[k][:, src0:src0 + n],
                                            in1=bias1[:, src0:src0 + n], op=ADD)

        def finish(w):
            half, v = divmod(w, 4)
            spans = [(1024 * v + 128, 1024 * v + 640)]
            if v < 3:
                spans.append((1024 * v + 640, 1024 * v + 1152))
            else:
                spans.extend([(3712, 4096), (0, 128)])
            for (a, b) in spans:
                piece = o_sb[half][:, a:b]
                nc.scalar.activation(out=piece, in_=piece, func=RELU)
                nc.sync.dma_start(out=out[128 * half:128 * half + 128, a:b], in_=piece)

        transpose_inputs(0)
        copy_inputs(0)
        biases()
        regroup_weights(0)
        regroup_weights(1)
        quantise_weights(0)
        quantise_inputs(0)
        regroup_weights(2)
        quantise_weights(1)
        quantise_weights(2)
        transpose_inputs(1)
        copy_inputs(1)
        quantise_inputs(1)

        for s in range(UNITS + LAG_OUT):
            if s + AHEAD_X < UNITS:
                transpose_inputs(s + AHEAD_X)
                copy_inputs(s + AHEAD_X)
            if s < UNITS:
                layer1(s)
            if 0 <= s - LAG_H < UNITS:
                regroup_h(s - LAG_H)
            if s == 0:
                regroup_weights(3)
            if s + AHEAD_X < UNITS:
                quantise_inputs(s + AHEAD_X)
            if s == 0:
                quantise_weights(3)
            if 0 <= s - LAG_H < UNITS:
                quantise_h(s - LAG_H)
            if 0 <= s - LAG_Y < UNITS:
                layer2(s - LAG_Y)
            if 0 <= s - LAG_OUT < UNITS:
                finish(s - LAG_OUT)
